import numpy as np
import ml_dtypes


def mxq(x, axis, fmt="e4m3"):
    dtype, down = {"e4m3": (ml_dtypes.float8_e4m3fn, 7), "e5m2": (ml_dtypes.float8_e5m2, 14)}[fmt]
    v = np.moveaxis(np.asarray(x, np.float32).astype(ml_dtypes.bfloat16).astype(np.float64), axis, -1)
    blocks = v.reshape(v.shape[:-1] + (-1, 32))
    amax = np.abs(blocks).max(-1, keepdims=True)
    byte = np.maximum(np.where(amax > 0, np.frexp(amax)[1] - 1 + 127, 0) - down, 1)
    scale = np.exp2(byte - 127.0)
    codes = (blocks / scale).astype(np.float32).astype(dtype).astype(np.float64)
    return np.moveaxis((codes * scale).reshape(v.shape), -1, axis)


WIDE = False


def mx_kscale(k):
    if not WIDE:
        return np.ones(k)
    levels = np.array([10, -10, 5, -5, 0])
    a = np.random.permutation(np.resize(levels, k // 512 * 4)).reshape(k // 512, 4)
    idx = np.arange(k)
    return np.exp2(a[idx // 512, idx % 128 // 32])


BF16 = ml_dtypes.bfloat16


def bf(x):
    return np.asarray(x, np.float32).astype(BF16)


def f64(x):
    return np.asarray(x).astype(np.float64)


T, H, F = 256, 1024, 3584


def silu(v):
    return v / (1.0 + np.exp(-v))


def setup_inputs():
    s, t = mx_kscale(H), mx_kscale(F)
    return {"x": bf(np.random.standard_normal((T, H)) * s),
            "expert_w1": bf(np.random.standard_normal((H, F)) * 0.03125 / s[:, None]),
            "expert_v1": bf(np.random.standard_normal((H, F)) * 0.03125 / s[:, None] * t),
            "expert_w2": bf(np.random.standard_normal((H, F)) * 0.03 / t[None, :])}


def reference(x, expert_w1, expert_v1, expert_w2):
    xq = mxq(f64(x), 1, "e4m3")
    gate_proj = silu(xq @ mxq(f64(expert_w1), 0, "e4m3"))
    up_proj = xq @ mxq(f64(expert_v1), 0, "e4m3")
    h = gate_proj * up_proj
    down_proj = mxq(h, 1, "e4m3") @ mxq(f64(expert_w2), 1, "e4m3").T
    return down_proj

@@ -1,0 +1,267 @@
+from contextlib import ExitStack
+
+import concourse.mybir as mybir
+from concourse.masks import make_identity
+
+F32 = mybir.dt.float32
+BF16 = mybir.dt.bfloat16
+U32 = mybir.dt.uint32
+U8 = mybir.dt.uint8
+FP8X4 = mybir.dt.float8_e4m3fn_x4
+SILU = mybir.ActivationFunctionType.Silu
+MULT = mybir.AluOpType.mult
+
+P = 128
+T, H, F = 256, 1024, 3584
+KP = 512
+NG = F // KP
+FLOPS = 2 * T * H * F * 3
+
+A_CHUNKS = ((0, 1), (1, 2), (3, 2), (5, 2))
+B_CHUNKS = ((0, 2), (2, 2), (4, 2), (6, 1))
+ORDER = (("A", 0), ("A", 1), ("B", 0), ("A", 2), ("B", 1), ("A", 3), ("B", 2), ("B", 3))
+A_BUFS = 6
+B_BUFS = 2
+EV_ON_VECTOR_EVERY = 6
+
+
+def tile_dbrxexpertglu_kernel(tc, x, expert_w1, expert_v1, expert_w2, out):
+    nc = tc.nc
+    with ExitStack() as ctx:
+        keep = ctx.enter_context(tc.tile_pool(name="keep", bufs=1))
+        araw_pool = ctx.enter_context(tc.tile_pool(name="araw", bufs=A_BUFS))
+        braw_pool = ctx.enter_context(tc.tile_pool(name="braw", bufs=B_BUFS))
+        agrp_pool = ctx.enter_context(tc.tile_pool(name="agrp", bufs=4))
+        bgrp_pool = ctx.enter_context(tc.tile_pool(name="bgrp", bufs=3))
+        acode_pool = ctx.enter_context(tc.tile_pool(name="acode", bufs=2))
+        bcode_pool = ctx.enter_context(tc.tile_pool(name="bcode", bufs=3))
+        sg_pool = ctx.enter_context(tc.tile_pool(name="sgp", bufs=4))
+        hg_pool = ctx.enter_context(tc.tile_pool(name="hgp", bufs=2))
+        ost_pool = ctx.enter_context(tc.tile_pool(name="ost", bufs=4))
+        acc_pool = ctx.enter_context(tc.psum_pool(name="accp", bufs=1))
+        gu_pool = ctx.enter_context(tc.psum_pool(name="gup", bufs=1))
+        tr_pool = ctx.enter_context(tc.psum_pool(name="trp", bufs=2))
+
+        ident = keep.tile([P, P], F32, name="ident")
+        make_identity(nc, ident[:])
+
+        x_raw = keep.tile([P, 2 * H], BF16, name="x_raw")
+        nc.sync.dma_start(
+            out=x_raw[:].rearrange("p (a k) -> p a k", a=2),
+            in_=x.rearrange("(a p) k -> p a k", p=P),
+        )
+
+        pending = []
+        for kind, idx in ORDER:
+            if kind == "A":
+                for m in range(2):
+                    for c in range(2):
+                        pending.append(("A", idx, m, c))
+            else:
+                pending.append(("B", idx, 0, 0))
+        loaded = {}
+        live = {"A": 0, "B": 0}
+        limit = {"A": A_BUFS, "B": B_BUFS}
+
+        issued = [0]
+
+        def pump():
+            while issued[0] < len(pending) and live[pending[issued[0]][0]] < limit[pending[issued[0]][0]]:
+                kind, idx, m, c = pending[issued[0]]
+                issued[0] += 1
+                live[kind] += 1
+                if kind == "A":
+                    g0, n = A_CHUNKS[idx]
+                    width = n * KP
+                    w = expert_w1 if m == 0 else expert_v1
+                    piece = araw_pool.tile([P, 4 * width], BF16, name="araw")
+                    nc.sync.dma_start(
+                        out=piece[:].rearrange("p (j w) -> p j w", j=4),
+                        in_=w[c * KP : (c + 1) * KP, g0 * KP : g0 * KP + width].rearrange(
+                            "(p j) w -> p j w", j=4
+                        ),
+                    )
+                else:
+                    g0, n = B_CHUNKS[idx]
+                    width = n * KP
+                    piece = braw_pool.tile([P, 8 * width], BF16, name="braw")
+                    nc.sync.dma_start(
+                        out=piece[:].rearrange("p (o w) -> p o w", o=8),
+                        in_=expert_w2[:, g0 * KP : g0 * KP + width].rearrange(
+                            "(o p) w -> p o w", p=P
+                        ),
+                    )
+                loaded[(kind, idx, m, c)] = piece
+
+        pump()
+
+        x_grp = keep.tile([P, 2 * T * 4], BF16, name="x_grp", align_bytes=64)
+        x_codes = keep.tile([P, 2 * T], U32, name="x_codes", align_bytes=64)
+        x_scales = keep.tile([P, 2 * T], U8, name="x_scales", align_bytes=64)
+        x_words = x_raw[:].bitcast(F32).rearrange("p (a c m u) -> p a c u m", a=2, c=2, u=2)
+        x_grp_words = x_grp[:].bitcast(F32)
+        for c in range(2):
+            bank = tr_pool.tile([P, 512], F32, name="tr")
+            for a in range(2):
+                for u in range(2):
+                    s = a * 2 + u
+                    nc.tensor.transpose(bank[:, s * P : (s + 1) * P], x_words[:, a, c, u, :], ident[:])
+            nc.scalar.copy(
+                out=x_grp_words[:, c * 512 : (c + 1) * 512].rearrange(
+                    "p (a t u) -> p a t u", a=2, u=2
+                ),
+                in_=bank[:].rearrange("p (a u t) -> p a t u", a=2, u=2),
+            )
+        nc.vector.quantize_mx(out=x_codes[:].bitcast(FP8X4), scales=x_scales[:], in_=x_grp[:])
+
+        h_codes = keep.tile([P, NG * T], U32, name="h_codes", align_bytes=64)
+        h_scales = keep.tile([P, NG * T], U8, name="h_scales", align_bytes=64)
+        acc = [
+            [acc_pool.tile([P, 512], F32, name="acc%d%d" % (tt, ob)) for ob in range(2)]
+            for tt in range(2)
+        ]
+
+        def stage1(bank, codes, scales, n, gi, th):
+            for j4 in range(4):
+                for c in range(2):
+                    col = (c * n + gi) * KP + j4 * P
+                    xcol = c * T + th * P
+                    nc.tensor.matmul_mx(
+                        out=bank[:, j4 * P : (j4 + 1) * P],
+                        lhsT=codes[:, col : col + P].bitcast(FP8X4),
+                        lhsT_scale=scales[:, col : col + P],
+                        rhs=x_codes[:, xcol : xcol + P].bitcast(FP8X4),
+                        rhs_scale=x_scales[:, xcol : xcol + P],
+                        start=(c == 0),
+                        stop=(c == 1),
+                    )
+
+        def a_chunk(idx):
+            g0, n = A_CHUNKS[idx]
+            width = n * KP
+            silus = {}
+            for m in range(2):
+                codes = acode_pool.tile([P, 2 * n * KP], U32, name="acodes%d" % m, align_bytes=64)
+                scales = acode_pool.tile([P, 2 * n * KP], U8, name="ascales%d" % m, align_bytes=64)
+                for c in range(2):
+                    piece = loaded[("A", idx, m, c)]
+                    rows = piece[:].rearrange("p (j w) -> p j w", j=4)
+                    for gi in range(n):
+                        grp = agrp_pool.tile([P, 4 * KP], BF16, name="agrp", align_bytes=64)
+                        for u in range(2):
+                            lo = gi * KP + u * 256
+                            copy = nc.vector.tensor_copy if u == 0 else nc.scalar.copy
+                            copy(
+                                out=grp[:, u * 1024 : (u + 1) * 1024].rearrange(
+                                    "p (e q j) -> p q e j", e=2, j=4
+                                ),
+                                in_=rows[:, :, lo : lo + 256].rearrange("p j (q e) -> p q e j", e=2),
+                            )
+                        col = (c * n + gi) * KP
+                        nc.vector.quantize_mx(
+                            out=codes[:, col : col + KP].bitcast(FP8X4),
+                            scales=scales[:, col : col + KP],
+                            in_=grp[:],
+                        )
+                    live["A"] -= 1
+                    pump()
+                for gi in range(n):
+                    if m == 1:
+                        hg = hg_pool.tile([P, 2 * 512], BF16, name="hg", align_bytes=64)
+                    for th in range(2):
+                        if m == 0:
+                            gate = gu_pool.tile([P, 512], F32, name="gate")
+                            stage1(gate, codes, scales, n, gi, th)
+                            sg = sg_pool.tile([P, 512], F32, name="sg")
+                            nc.scalar.activation(
+                                out=sg[:].rearrange("p (t j) -> p t j", j=4),
+                                in_=gate[:].rearrange("p (j t) -> p t j", j=4),
+                                func=SILU,
+                            )
+                            silus[(gi, th)] = sg
+                        else:
+                            up = gu_pool.tile([P, 512], F32, name="up")
+                            stage1(up, codes, scales, n, gi, th)
+                            nc.vector.tensor_tensor(
+                                out=hg[:, th * 512 : (th + 1) * 512].rearrange(
+                                    "p (t j) -> p t j", j=4
+                                ),
+                                in0=silus[(gi, th)][:].rearrange("p (t j) -> p t j", j=4),
+                                in1=up[:].rearrange("p (j t) -> p t j", j=4),
+                                op=MULT,
+                            )
+                    if m == 1:
+                        g = g0 + gi
+                        nc.vector.quantize_mx(
+                            out=h_codes[:, g * T : (g + 1) * T].bitcast(FP8X4),
+                            scales=h_scales[:, g * T : (g + 1) * T],
+                            in_=hg[:],
+                        )
+
+        ev_count = [0]
+
+        def b_chunk(idx):
+            g0, n = B_CHUNKS[idx]
+            half = n * KP // 2
+            piece = loaded[("B", idx, 0, 0)]
+            words = piece[:].bitcast(F32)
+            for gi in range(n):
+                g = g0 + gi
+                codes = bcode_pool.tile([P, 1024], U32, name="bcodes", align_bytes=64)
+                scales = bcode_pool.tile([P, 1024], U8, name="bscales", align_bytes=64)
+                for ob in range(2):
+                    grp = bgrp_pool.tile([P, 2048], BF16, name="bgrp", align_bytes=64)
+                    grp_words = grp[:].bitcast(F32)
+                    for b in range(2):
+                        bank = tr_pool.tile([P, 512], F32, name="tr")
+                        for a in range(2):
+                            ot = ob * 4 + b * 2 + a
+                            for u in range(2):
+                                s = a * 2 + u
+                                first = ot * half + gi * 256 + u * P
+                                nc.tensor.transpose(
+                                    bank[:, s * P : (s + 1) * P], words[:, first : first + P], ident[:]
+                                )
+                        ev_count[0] += 1
+                        on_vector = ev_count[0] % EV_ON_VECTOR_EVERY == 0
+                        copy = nc.vector.tensor_copy if on_vector else nc.scalar.copy
+                        copy(
+                            out=grp_words[:, b * 512 : (b + 1) * 512].rearrange(
+                                "p (a o u) -> p a o u", a=2, u=2
+                            ),
+                            in_=bank[:].rearrange("p (a u o) -> p a o u", a=2, u=2),
+                        )
+                    nc.vector.quantize_mx(
+                        out=codes[:, ob * 512 : (ob + 1) * 512].bitcast(FP8X4),
+                        scales=scales[:, ob * 512 : (ob + 1) * 512],
+                        in_=grp[:],
+                    )
+                for tt in range(2):
+                    for ob in range(2):
+                        hcol = g * T + tt * P
+                        nc.tensor.matmul_mx(
+                            out=acc[tt][ob][:],
+                            lhsT=h_codes[:, hcol : hcol + P].bitcast(FP8X4),
+                            lhsT_scale=h_scales[:, hcol : hcol + P],
+                            rhs=codes[:, ob * 512 : (ob + 1) * 512].bitcast(FP8X4),
+                            rhs_scale=scales[:, ob * 512 : (ob + 1) * 512],
+                            start=(g == 0),
+                            stop=(g == NG - 1),
+                        )
+            live["B"] -= 1
+            pump()
+
+        for kind, idx in ORDER:
+            if kind == "A":
+                a_chunk(idx)
+            else:
+                b_chunk(idx)
+
+        for tt in range(2):
+            for ob in range(2):
+                res = ost_pool.tile([P, 512], F32, name="res")
+                copy = nc.vector.tensor_copy if ob == 0 else nc.scalar.copy
+                copy(out=res[:], in_=acc[tt][ob][:])
+                nc.sync.dma_start(
+                    out=out[tt * P : (tt + 1) * P, ob * 512 : (ob + 1) * 512], in_=res[:]
+                )

@@ -15,18 +15,111 @@ P = 128
 T, H, F = 256, 1024, 3584
 KP = 512
 NG = F // KP
-FLOPS = 2 * T * H * F * 3
 
-A_CHUNKS = ((0, 1), (1, 2), (3, 2), (5, 2))
+A_CHUNKS = ((0, 2), (2, 2), (4, 2), (6, 1))
 B_CHUNKS = ((0, 2), (2, 2), (4, 2), (6, 1))
-ORDER = (("A", 0), ("A", 1), ("B", 0), ("A", 2), ("B", 1), ("A", 3), ("B", 2), ("B", 3))
-A_BUFS = 6
-B_BUFS = 2
-EV_ON_VECTOR_EVERY = 6
+B_AFTER = (5, 7, 9, 11, 12, 16, 16, 16)
+BANK_NUM, BANK_DEN = 2, 3
+DELTA = 0
+QS = 80
+LAG_G, LAG_S, LAG_U, LAG_M, LAG_QH, LAG_QB, LAG_S2, TR_LEAD = 1, 1, 1, 2, 1, 1, 2, 1
+MANUAL = True
+A_BUFS = 8
+B_BUFS = 4
+
+
+def make_plan():
+    pieces = []
+    units = []
+    first_step = []
+    for idx, (g0, n) in enumerate(A_CHUNKS):
+        for m in range(2):
+            for c in range(2):
+                pieces.append(("A", idx, m, c))
+                first_step.append(len(units))
+                for k in range(n):
+                    units.append((idx, m, c, g0 + k, k, k == n - 1))
+    first_step.append(len(units))
+    b_pieces = []
+    banks = []
+    for idx, (g0, n) in enumerate(B_CHUNKS):
+        for ob in range(2):
+            b_pieces.append(("B", idx, ob, n))
+            for k in range(n):
+                for b in range(2):
+                    banks.append((idx, g0 + k, k, ob, b, k == n - 1 and b == 1))
+    loads = []
+    nxt = 0
+    for a in range(len(pieces) + 1):
+        while nxt < len(b_pieces) and B_AFTER[nxt] == a:
+            loads.append(b_pieces[nxt])
+            nxt += 1
+        if a < len(pieces):
+            loads.append(pieces[a])
+    bank_step = []
+    cur = -1000000
+    for j, piece in enumerate(b_pieces):
+        cur = max(cur, (first_step[B_AFTER[j]] + DELTA) * BANK_DEN)
+        for k in range(piece[3] * 2):
+            bank_step.append(cur // BANK_DEN)
+            cur += BANK_NUM
+
+    due = {}
+
+    def add(step, slot, op):
+        if (step, slot) not in due:
+            due[(step, slot)] = []
+        due[(step, slot)].append(op)
+
+    unit_step = {}
+    for s, (idx, m, c, g, k, last) in enumerate(units):
+        unit_step[(g, m, c)] = s
+    silu_step = {}
+    qh_step = {}
+    prev = -9
+    for g in range(NG):
+        for th in range(2):
+            gs = max(unit_step[(g, 0, 1)] + LAG_G, prev)
+            add(gs, "pe_gate", ("GU", g, 0, th))
+            prev = gs + LAG_S
+            add(prev, "s_silu", ("SILU", g, th))
+            silu_step[(g, th)] = prev
+    prev = -9
+    for g in range(NG):
+        for th in range(2):
+            us = max(unit_step[(g, 1, 1)] + LAG_U, prev, silu_step[(g, th)] - LAG_M)
+            add(us, "pe_up", ("GU", g, 1, th))
+            prev = us + LAG_M
+            add(prev, "v_mul", ("MUL", g, th))
+            add(prev + LAG_QH, "v_q", ("QH", g, th))
+            qh_step[(g, th)] = prev + LAG_QH
+    qb_step = {}
+    for t, (idx, g, k, ob, b, last) in enumerate(banks):
+        s = bank_step[t]
+        early = bank_step[t - 2] + 1 if t >= 2 else -1
+        add(max(s - TR_LEAD, early, -1), "pe_tr", ("TR", idx, g, k, ob, b, last))
+        add(s, "s_ev", ("EV", g, ob, b))
+        if b == 1:
+            add(s + LAG_QB, "v_q", ("QB", g, ob))
+            qb_step[(g, ob)] = s + LAG_QB
+    last_s2 = {}
+    for g in range(NG):
+        for tt in range(2):
+            for ob in range(2):
+                s = max(qb_step[(g, ob)], qh_step[(g, tt)]) + LAG_S2
+                s = max(s, last_s2.get((tt, ob), -99))
+                last_s2[(tt, ob)] = s
+                add(s, "pe_s2", ("S2", g, tt, ob))
+    n_steps = max(step for step, slot in due) + 1
+    return loads, units, due, n_steps
+
+
+FLOPS = 2 * T * H * F * 3
 
 
 def tile_dbrxexpertglu_kernel(tc, x, expert_w1, expert_v1, expert_w2, out):
     nc = tc.nc
+    loads, units, due, n_steps = make_plan()
     with ExitStack() as ctx:
         keep = ctx.enter_context(tc.tile_pool(name="keep", bufs=1))
         araw_pool = ctx.enter_context(tc.tile_pool(name="araw", bufs=A_BUFS))
@@ -41,6 +134,8 @@ def tile_dbrxexpertglu_kernel(tc, x, expert_w1, expert_v1, expert_w2, out):
         acc_pool = ctx.enter_context(tc.psum_pool(name="accp", bufs=1))
         gu_pool = ctx.enter_context(tc.psum_pool(name="gup", bufs=1))
         tr_pool = ctx.enter_context(tc.psum_pool(name="trp", bufs=2))
+        if MANUAL:
+            ctx.enter_context(tc.manual_schedule())
 
         ident = keep.tile([P, P], F32, name="ident")
         make_identity(nc, ident[:])
@@ -51,26 +146,18 @@ def tile_dbrxexpertglu_kernel(tc, x, expert_w1, expert_v1, expert_w2, out):
             in_=x.rearrange("(a p) k -> p a k", p=P),
         )
 
-        pending = []
-        for kind, idx in ORDER:
-            if kind == "A":
-                for m in range(2):
-                    for c in range(2):
-                        pending.append(("A", idx, m, c))
-            else:
-                pending.append(("B", idx, 0, 0))
-        loaded = {}
+        raw = {}
         live = {"A": 0, "B": 0}
         limit = {"A": A_BUFS, "B": B_BUFS}
-
         issued = [0]
 
         def pump():
-            while issued[0] < len(pending) and live[pending[issued[0]][0]] < limit[pending[issued[0]][0]]:
-                kind, idx, m, c = pending[issued[0]]
+            while issued[0] < len(loads) and live[loads[issued[0]][0]] < limit[loads[issued[0]][0]]:
+                kind, idx, second, third = loads[issued[0]]
                 issued[0] += 1
                 live[kind] += 1
                 if kind == "A":
+                    m, c = second, third
                     g0, n = A_CHUNKS[idx]
                     width = n * KP
                     w = expert_w1 if m == 0 else expert_v1
@@ -81,17 +168,19 @@ def tile_dbrxexpertglu_kernel(tc, x, expert_w1, expert_v1, expert_w2, out):
                             "(p j) w -> p j w", j=4
                         ),
                     )
+                    raw[("A", idx, m, c)] = piece
                 else:
+                    ob = second
                     g0, n = B_CHUNKS[idx]
                     width = n * KP
-                    piece = braw_pool.tile([P, 8 * width], BF16, name="braw")
+                    piece = braw_pool.tile([P, 4 * width], BF16, name="braw")
                     nc.sync.dma_start(
-                        out=piece[:].rearrange("p (o w) -> p o w", o=8),
-                        in_=expert_w2[:, g0 * KP : g0 * KP + width].rearrange(
-                            "(o p) w -> p o w", p=P
-                        ),
+                        out=piece[:].rearrange("p (o w) -> p o w", o=4),
+                        in_=expert_w2[
+                            ob * 512 : (ob + 1) * 512, g0 * KP : g0 * KP + width
+                        ].rearrange("(o p) w -> p o w", p=P),
                     )
-                loaded[(kind, idx, m, c)] = piece
+                    raw[("B", idx, ob)] = piece
 
         pump()
 
@@ -121,141 +210,183 @@ def tile_dbrxexpertglu_kernel(tc, x, expert_w1, expert_v1, expert_w2, out):
             for tt in range(2)
         ]
 
-        def stage1(bank, codes, scales, n, gi, th):
-            for j4 in range(4):
-                for c in range(2):
-                    col = (c * n + gi) * KP + j4 * P
-                    xcol = c * T + th * P
-                    nc.tensor.matmul_mx(
-                        out=bank[:, j4 * P : (j4 + 1) * P],
-                        lhsT=codes[:, col : col + P].bitcast(FP8X4),
-                        lhsT_scale=scales[:, col : col + P],
-                        rhs=x_codes[:, xcol : xcol + P].bitcast(FP8X4),
-                        rhs_scale=x_scales[:, xcol : xcol + P],
-                        start=(c == 0),
-                        stop=(c == 1),
-                    )
+        tiles = {}
 
-        def a_chunk(idx):
-            g0, n = A_CHUNKS[idx]
-            width = n * KP
-            silus = {}
-            for m in range(2):
-                codes = acode_pool.tile([P, 2 * n * KP], U32, name="acodes%d" % m, align_bytes=64)
-                scales = acode_pool.tile([P, 2 * n * KP], U8, name="ascales%d" % m, align_bytes=64)
-                for c in range(2):
-                    piece = loaded[("A", idx, m, c)]
-                    rows = piece[:].rearrange("p (j w) -> p j w", j=4)
-                    for gi in range(n):
-                        grp = agrp_pool.tile([P, 4 * KP], BF16, name="agrp", align_bytes=64)
-                        for u in range(2):
-                            lo = gi * KP + u * 256
-                            copy = nc.vector.tensor_copy if u == 0 else nc.scalar.copy
-                            copy(
-                                out=grp[:, u * 1024 : (u + 1) * 1024].rearrange(
-                                    "p (e q j) -> p q e j", e=2, j=4
-                                ),
-                                in_=rows[:, :, lo : lo + 256].rearrange("p j (q e) -> p q e j", e=2),
-                            )
-                        col = (c * n + gi) * KP
-                        nc.vector.quantize_mx(
-                            out=codes[:, col : col + KP].bitcast(FP8X4),
-                            scales=scales[:, col : col + KP],
-                            in_=grp[:],
-                        )
-                    live["A"] -= 1
-                    pump()
-                for gi in range(n):
-                    if m == 1:
-                        hg = hg_pool.tile([P, 2 * 512], BF16, name="hg", align_bytes=64)
-                    for th in range(2):
-                        if m == 0:
-                            gate = gu_pool.tile([P, 512], F32, name="gate")
-                            stage1(gate, codes, scales, n, gi, th)
-                            sg = sg_pool.tile([P, 512], F32, name="sg")
-                            nc.scalar.activation(
-                                out=sg[:].rearrange("p (t j) -> p t j", j=4),
-                                in_=gate[:].rearrange("p (j t) -> p t j", j=4),
-                                func=SILU,
-                            )
-                            silus[(gi, th)] = sg
-                        else:
-                            up = gu_pool.tile([P, 512], F32, name="up")
-                            stage1(up, codes, scales, n, gi, th)
-                            nc.vector.tensor_tensor(
-                                out=hg[:, th * 512 : (th + 1) * 512].rearrange(
-                                    "p (t j) -> p t j", j=4
-                                ),
-                                in0=silus[(gi, th)][:].rearrange("p (t j) -> p t j", j=4),
-                                in1=up[:].rearrange("p (j t) -> p t j", j=4),
-                                op=MULT,
-                            )
-                    if m == 1:
-                        g = g0 + gi
-                        nc.vector.quantize_mx(
-                            out=h_codes[:, g * T : (g + 1) * T].bitcast(FP8X4),
-                            scales=h_scales[:, g * T : (g + 1) * T],
-                            in_=hg[:],
-                        )
+        def regroup_views(unit):
+            idx, m, c, g, k, last = unit
+            if ("agrp", g, m, c) not in tiles:
+                tiles[("agrp", g, m, c)] = agrp_pool.tile(
+                    [P, 4 * KP], BF16, name="agrp", align_bytes=64
+                )
+            grp = tiles[("agrp", g, m, c)]
+            rows = raw[("A", idx, m, c)][:].rearrange("p (j w) -> p j w", j=4)
+            src = rows[:, :, k * KP : (k + 1) * KP].rearrange("p j (u q e) -> p u q e j", u=2, e=2)
+            dst = grp[:].rearrange("p (u e q j) -> p u q e j", u=2, e=2, j=4)
+            return src, dst
 
-        ev_count = [0]
+        def regroup_v(unit):
+            src, dst = regroup_views(unit)
+            nc.vector.tensor_copy(out=dst[:, :, 0:QS, :, :], in_=src[:, :, 0:QS, :, :])
 
-        def b_chunk(idx):
-            g0, n = B_CHUNKS[idx]
-            half = n * KP // 2
-            piece = loaded[("B", idx, 0, 0)]
-            words = piece[:].bitcast(F32)
-            for gi in range(n):
-                g = g0 + gi
-                codes = bcode_pool.tile([P, 1024], U32, name="bcodes", align_bytes=64)
-                scales = bcode_pool.tile([P, 1024], U8, name="bscales", align_bytes=64)
-                for ob in range(2):
-                    grp = bgrp_pool.tile([P, 2048], BF16, name="bgrp", align_bytes=64)
-                    grp_words = grp[:].bitcast(F32)
-                    for b in range(2):
-                        bank = tr_pool.tile([P, 512], F32, name="tr")
-                        for a in range(2):
-                            ot = ob * 4 + b * 2 + a
-                            for u in range(2):
-                                s = a * 2 + u
-                                first = ot * half + gi * 256 + u * P
-                                nc.tensor.transpose(
-                                    bank[:, s * P : (s + 1) * P], words[:, first : first + P], ident[:]
-                                )
-                        ev_count[0] += 1
-                        on_vector = ev_count[0] % EV_ON_VECTOR_EVERY == 0
-                        copy = nc.vector.tensor_copy if on_vector else nc.scalar.copy
-                        copy(
-                            out=grp_words[:, b * 512 : (b + 1) * 512].rearrange(
-                                "p (a o u) -> p a o u", a=2, u=2
-                            ),
-                            in_=bank[:].rearrange("p (a u o) -> p a o u", a=2, u=2),
-                        )
-                    nc.vector.quantize_mx(
-                        out=codes[:, ob * 512 : (ob + 1) * 512].bitcast(FP8X4),
-                        scales=scales[:, ob * 512 : (ob + 1) * 512],
-                        in_=grp[:],
-                    )
-                for tt in range(2):
-                    for ob in range(2):
-                        hcol = g * T + tt * P
+        def regroup_s(unit, u):
+            src, dst = regroup_views(unit)
+            nc.scalar.copy(out=dst[:, u, QS:P, :, :], in_=src[:, u, QS:P, :, :])
+
+        def a_codes(idx, m):
+            n = A_CHUNKS[idx][1]
+            if ("acodes", idx, m) not in tiles:
+                tiles[("acodes", idx, m)] = acode_pool.tile(
+                    [P, 2 * n * KP], U32, name="acodes%d" % m, align_bytes=64
+                )
+                tiles[("ascales", idx, m)] = acode_pool.tile(
+                    [P, 2 * n * KP], U8, name="ascales%d" % m, align_bytes=64
+                )
+            return tiles[("acodes", idx, m)], tiles[("ascales", idx, m)], n
+
+        def quantise_a(unit):
+            idx, m, c, g, k, last = unit
+            codes, scales, n = a_codes(idx, m)
+            col = (c * n + k) * KP
+            nc.vector.quantize_mx(
+                out=codes[:, col : col + KP].bitcast(FP8X4),
+                scales=scales[:, col : col + KP],
+                in_=tiles[("agrp", g, m, c)][:],
+            )
+
+        chunk_of = {}
+        for idx, (g0, n) in enumerate(A_CHUNKS):
+            for k in range(n):
+                chunk_of[g0 + k] = (idx, k)
+
+        def emit(op):
+            kind = op[0]
+            if kind == "GU":
+                g, m, th = op[1:]
+                idx, k = chunk_of[g]
+                codes, scales, n = a_codes(idx, m)
+                bank = gu_pool.tile([P, 512], F32, name="gate" if m == 0 else "up")
+                tiles[("gu", g, m, th)] = bank
+                for j4 in range(4):
+                    for c in range(2):
+                        col = (c * n + k) * KP + j4 * P
+                        xcol = c * T + th * P
                         nc.tensor.matmul_mx(
-                            out=acc[tt][ob][:],
-                            lhsT=h_codes[:, hcol : hcol + P].bitcast(FP8X4),
-                            lhsT_scale=h_scales[:, hcol : hcol + P],
-                            rhs=codes[:, ob * 512 : (ob + 1) * 512].bitcast(FP8X4),
-                            rhs_scale=scales[:, ob * 512 : (ob + 1) * 512],
-                            start=(g == 0),
-                            stop=(g == NG - 1),
+                            out=bank[:, j4 * P : (j4 + 1) * P],
+                            lhsT=codes[:, col : col + P].bitcast(FP8X4),
+                            lhsT_scale=scales[:, col : col + P],
+                            rhs=x_codes[:, xcol : xcol + P].bitcast(FP8X4),
+                            rhs_scale=x_scales[:, xcol : xcol + P],
+                            start=(c == 0),
+                            stop=(c == 1),
                         )
-            live["B"] -= 1
-            pump()
-
-        for kind, idx in ORDER:
-            if kind == "A":
-                a_chunk(idx)
+            elif kind == "SILU":
+                g, th = op[1:]
+                sg = sg_pool.tile([P, 512], F32, name="sg")
+                tiles[("sg", g, th)] = sg
+                nc.scalar.activation(
+                    out=sg[:].rearrange("p (t j) -> p t j", j=4),
+                    in_=tiles[("gu", g, 0, th)][:].rearrange("p (j t) -> p t j", j=4),
+                    func=SILU,
+                )
+            elif kind == "MUL":
+                g, th = op[1:]
+                if th == 0:
+                    tiles[("hg", g)] = hg_pool.tile([P, 2 * 512], BF16, name="hg", align_bytes=64)
+                nc.vector.tensor_tensor(
+                    out=tiles[("hg", g)][:, th * 512 : (th + 1) * 512].rearrange(
+                        "p (t j) -> p t j", j=4
+                    ),
+                    in0=tiles[("sg", g, th)][:].rearrange("p (t j) -> p t j", j=4),
+                    in1=tiles[("gu", g, 1, th)][:].rearrange("p (j t) -> p t j", j=4),
+                    op=MULT,
+                )
+            elif kind == "QH":
+                g, th = op[1:]
+                col = g * T + th * P
+                nc.vector.quantize_mx(
+                    out=h_codes[:, col : col + P].bitcast(FP8X4),
+                    scales=h_scales[:, col : col + P],
+                    in_=tiles[("hg", g)][:, th * 512 : (th + 1) * 512],
+                )
+            elif kind == "TR":
+                idx, g, k, ob, b, last = op[1:]
+                half = B_CHUNKS[idx][1] * KP // 2
+                words = raw[("B", idx, ob)][:].bitcast(F32)
+                bank = tr_pool.tile([P, 512], F32, name="tr")
+                tiles[("tr", g, ob, b)] = bank
+                for a in range(2):
+                    for u in range(2):
+                        s = a * 2 + u
+                        first = (b * 2 + a) * half + k * 256 + u * P
+                        nc.tensor.transpose(
+                            bank[:, s * P : (s + 1) * P], words[:, first : first + P], ident[:]
+                        )
+                if last:
+                    live["B"] -= 1
+            elif kind == "EV":
+                g, ob, b = op[1:]
+                if b == 0:
+                    tiles[("bgrp", g, ob)] = bgrp_pool.tile(
+                        [P, 2048], BF16, name="bgrp", align_bytes=64
+                    )
+                nc.scalar.copy(
+                    out=tiles[("bgrp", g, ob)][:]
+                    .bitcast(F32)[:, b * 512 : (b + 1) * 512]
+                    .rearrange("p (a o u) -> p a o u", a=2, u=2),
+                    in_=tiles[("tr", g, ob, b)][:].rearrange("p (a u o) -> p a o u", a=2, u=2),
+                )
+            elif kind == "QB":
+                g, ob = op[1:]
+                if ("bcodes", g) not in tiles:
+                    tiles[("bcodes", g)] = bcode_pool.tile(
+                        [P, 1024], U32, name="bcodes", align_bytes=64
+                    )
+                    tiles[("bscales", g)] = bcode_pool.tile(
+                        [P, 1024], U8, name="bscales", align_bytes=64
+                    )
+                nc.vector.quantize_mx(
+                    out=tiles[("bcodes", g)][:, ob * 512 : (ob + 1) * 512].bitcast(FP8X4),
+                    scales=tiles[("bscales", g)][:, ob * 512 : (ob + 1) * 512],
+                    in_=tiles[("bgrp", g, ob)][:],
+                )
             else:
-                b_chunk(idx)
+                g, tt, ob = op[1:]
+                hcol = g * T + tt * P
+                nc.tensor.matmul_mx(
+                    out=acc[tt][ob][:],
+                    lhsT=h_codes[:, hcol : hcol + P].bitcast(FP8X4),
+                    lhsT_scale=h_scales[:, hcol : hcol + P],
+                    rhs=tiles[("bcodes", g)][:, ob * 512 : (ob + 1) * 512].bitcast(FP8X4),
+                    rhs_scale=tiles[("bscales", g)][:, ob * 512 : (ob + 1) * 512],
+                    start=(g == 0),
+                    stop=(g == NG - 1),
+                )
+
+        def run(step, slot):
+            for op in due.get((step, slot), []):
+                emit(op)
+
+        for step in range(-1, n_steps):
+            unit = units[step] if 0 <= step < len(units) else None
+            run(step, "pe_tr")
+            if unit is not None:
+                regroup_v(unit)
+            run(step, "v_mul")
+            if 1 <= step <= len(units):
+                quantise_a(units[step - 1])
+            run(step, "v_q")
+            if unit is not None:
+                regroup_s(unit, 0)
+            run(step, "s_ev")
+            if unit is not None:
+                regroup_s(unit, 1)
+            run(step, "s_silu")
+            if unit is not None and unit[5]:
+                live["A"] -= 1
+            run(step, "pe_s2")
+            run(step, "pe_up")
+            run(step, "pe_gate")
+            pump()
 
         for tt in range(2):
             for ob in range(2):

@@ -212,7 +212,7 @@ def tile_dbrxexpertglu_kernel(tc, x, expert_w1, expert_v1, expert_w2, out):
 
         tiles = {}
 
-        def regroup_views(unit):
+        def regroup_views(unit, u):
             idx, m, c, g, k, last = unit
             if ("agrp", g, m, c) not in tiles:
                 tiles[("agrp", g, m, c)] = agrp_pool.tile(
@@ -220,17 +220,23 @@ def tile_dbrxexpertglu_kernel(tc, x, expert_w1, expert_v1, expert_w2, out):
                 )
             grp = tiles[("agrp", g, m, c)]
             rows = raw[("A", idx, m, c)][:].rearrange("p (j w) -> p j w", j=4)
-            src = rows[:, :, k * KP : (k + 1) * KP].rearrange("p j (u q e) -> p u q e j", u=2, e=2)
-            dst = grp[:].rearrange("p (u e q j) -> p u q e j", u=2, e=2, j=4)
-            return src, dst
+            lo = k * KP + u * 256
+            return rows[:, :, lo : lo + 256], grp[:, u * 1024 : (u + 1) * 1024]
 
         def regroup_v(unit):
-            src, dst = regroup_views(unit)
-            nc.vector.tensor_copy(out=dst[:, :, 0:QS, :, :], in_=src[:, :, 0:QS, :, :])
+            for u in range(2):
+                src, dst = regroup_views(unit, u)
+                nc.vector.tensor_copy(
+                    out=dst.rearrange("p (e c l j) -> p c j l e", e=2, l=2, j=4)[:, 0 : QS // 2],
+                    in_=src.rearrange("p j (c l e) -> p c j l e", l=2, e=2)[:, 0 : QS // 2],
+                )
 
         def regroup_s(unit, u):
-            src, dst = regroup_views(unit)
-            nc.scalar.copy(out=dst[:, u, QS:P, :, :], in_=src[:, u, QS:P, :, :])
+            src, dst = regroup_views(unit, u)
+            nc.scalar.copy(
+                out=dst.rearrange("p (e q j) -> p q j e", e=2, j=4)[:, QS:P],
+                in_=src.rearrange("p j (q e) -> p q j e", e=2)[:, QS:P],
+            )
 
         def a_codes(idx, m):
             n = A_CHUNKS[idx][1]

@@ -24,6 +24,7 @@ DELTA = 0
 QS = 80
 LAG_G, LAG_S, LAG_U, LAG_M, LAG_QH, LAG_QB, LAG_S2, TR_LEAD = 1, 1, 1, 2, 1, 1, 2, 1
 MANUAL = True
+X_AFTER, X_STEP = 1, 3
 A_BUFS = 8
 B_BUFS = 4
 
@@ -140,11 +141,6 @@ def tile_dbrxexpertglu_kernel(tc, x, expert_w1, expert_v1, expert_w2, out):
         ident = keep.tile([P, P], F32, name="ident")
         make_identity(nc, ident[:])
 
-        x_raw = keep.tile([P, 2 * H], BF16, name="x_raw")
-        nc.sync.dma_start(
-            out=x_raw[:].rearrange("p (a k) -> p a k", a=2),
-            in_=x.rearrange("(a p) k -> p a k", p=P),
-        )
 
         raw = {}
         live = {"A": 0, "B": 0}
@@ -182,6 +178,14 @@ def tile_dbrxexpertglu_kernel(tc, x, expert_w1, expert_v1, expert_w2, out):
                     )
                     raw[("B", idx, ob)] = piece
 
+        limit["A"] = X_AFTER
+        pump()
+        limit["A"] = A_BUFS
+        x_raw = keep.tile([P, 2 * H], BF16, name="x_raw")
+        nc.sync.dma_start(
+            out=x_raw[:].rearrange("p (a k) -> p a k", a=2),
+            in_=x.rearrange("(a p) k -> p a k", p=P),
+        )
         pump()
 
         x_grp = keep.tile([P, 2 * T * 4], BF16, name="x_grp", align_bytes=64)
@@ -189,19 +193,21 @@ def tile_dbrxexpertglu_kernel(tc, x, expert_w1, expert_v1, expert_w2, out):
         x_scales = keep.tile([P, 2 * T], U8, name="x_scales", align_bytes=64)
         x_words = x_raw[:].bitcast(F32).rearrange("p (a c m u) -> p a c u m", a=2, c=2, u=2)
         x_grp_words = x_grp[:].bitcast(F32)
-        for c in range(2):
-            bank = tr_pool.tile([P, 512], F32, name="tr")
-            for a in range(2):
-                for u in range(2):
-                    s = a * 2 + u
-                    nc.tensor.transpose(bank[:, s * P : (s + 1) * P], x_words[:, a, c, u, :], ident[:])
-            nc.scalar.copy(
-                out=x_grp_words[:, c * 512 : (c + 1) * 512].rearrange(
-                    "p (a t u) -> p a t u", a=2, u=2
-                ),
-                in_=bank[:].rearrange("p (a u t) -> p a t u", a=2, u=2),
-            )
-        nc.vector.quantize_mx(out=x_codes[:].bitcast(FP8X4), scales=x_scales[:], in_=x_grp[:])
+        def x_transpose():
+            for c in range(2):
+                bank = tr_pool.tile([P, 512], F32, name="tr")
+                for a in range(2):
+                    for u in range(2):
+                        s = a * 2 + u
+                        nc.tensor.transpose(
+                            bank[:, s * P : (s + 1) * P], x_words[:, a, c, u, :], ident[:]
+                        )
+                nc.scalar.copy(
+                    out=x_grp_words[:, c * 512 : (c + 1) * 512].rearrange(
+                        "p (a t u) -> p a t u", a=2, u=2
+                    ),
+                    in_=bank[:].rearrange("p (a u t) -> p a t u", a=2, u=2),
+                )
 
         h_codes = keep.tile([P, NG * T], U32, name="h_codes", align_bytes=64)
         h_scales = keep.tile([P, NG * T], U8, name="h_scales", align_bytes=64)
@@ -212,7 +218,7 @@ def tile_dbrxexpertglu_kernel(tc, x, expert_w1, expert_v1, expert_w2, out):
 
         tiles = {}
 
-        def regroup_views(unit, u):
+        def regroup_views(unit):
             idx, m, c, g, k, last = unit
             if ("agrp", g, m, c) not in tiles:
                 tiles[("agrp", g, m, c)] = agrp_pool.tile(
@@ -220,22 +226,21 @@ def tile_dbrxexpertglu_kernel(tc, x, expert_w1, expert_v1, expert_w2, out):
                 )
             grp = tiles[("agrp", g, m, c)]
             rows = raw[("A", idx, m, c)][:].rearrange("p (j w) -> p j w", j=4)
-            lo = k * KP + u * 256
-            return rows[:, :, lo : lo + 256], grp[:, u * 1024 : (u + 1) * 1024]
+            return rows[:, :, k * KP : (k + 1) * KP], grp[:]
 
         def regroup_v(unit):
-            for u in range(2):
-                src, dst = regroup_views(unit, u)
-                nc.vector.tensor_copy(
-                    out=dst.rearrange("p (e c l j) -> p c j l e", e=2, l=2, j=4)[:, 0 : QS // 2],
-                    in_=src.rearrange("p j (c l e) -> p c j l e", l=2, e=2)[:, 0 : QS // 2],
-                )
+            src, dst = regroup_views(unit)
+            nc.vector.tensor_copy(
+                out=dst.rearrange("p (e c l j) -> p c j l e", e=2, l=2, j=4)[:, 0 : QS],
+                in_=src.rearrange("p j (c l e) -> p c j l e", l=2, e=2)[:, 0 : QS],
+            )
 
-        def regroup_s(unit, u):
-            src, dst = regroup_views(unit, u)
+        def regroup_s(unit, part):
+            src, dst = regroup_views(unit)
+            lo = 2 * QS + part * (P - QS)
             nc.scalar.copy(
-                out=dst.rearrange("p (e q j) -> p q j e", e=2, j=4)[:, QS:P],
-                in_=src.rearrange("p j (q e) -> p q j e", e=2)[:, QS:P],
+                out=dst.rearrange("p (e q j) -> p q j e", e=2, j=4)[:, lo : lo + P - QS],
+                in_=src.rearrange("p j (q e) -> p q j e", e=2)[:, lo : lo + P - QS],
             )
 
         def a_codes(idx, m):
@@ -274,7 +279,7 @@ def tile_dbrxexpertglu_kernel(tc, x, expert_w1, expert_v1, expert_w2, out):
                 tiles[("gu", g, m, th)] = bank
                 for j4 in range(4):
                     for c in range(2):
-                        col = (c * n + k) * KP + j4 * P
+                        col = (c * n + k) * KP + ((j4 % 2) * 2 + j4 // 2) * P
                         xcol = c * T + th * P
                         nc.tensor.matmul_mx(
                             out=bank[:, j4 * P : (j4 + 1) * P],
@@ -374,6 +379,8 @@ def tile_dbrxexpertglu_kernel(tc, x, expert_w1, expert_v1, expert_w2, out):
 
         for step in range(-1, n_steps):
             unit = units[step] if 0 <= step < len(units) else None
+            if step == X_STEP - 1:
+                x_transpose()
             run(step, "pe_tr")
             if unit is not None:
                 regroup_v(unit)
@@ -381,6 +388,10 @@ def tile_dbrxexpertglu_kernel(tc, x, expert_w1, expert_v1, expert_w2, out):
             if 1 <= step <= len(units):
                 quantise_a(units[step - 1])
             run(step, "v_q")
+            if step == X_STEP:
+                nc.vector.quantize_mx(
+                    out=x_codes[:].bitcast(FP8X4), scales=x_scales[:], in_=x_grp[:]
+                )
             if unit is not None:
                 regroup_s(unit, 0)
             run(step, "s_ev")

@@ -25,6 +25,7 @@ QS = 80
 LAG_G, LAG_S, LAG_U, LAG_M, LAG_QH, LAG_QB, LAG_S2, TR_LEAD = 1, 1, 1, 2, 1, 1, 2, 1
 MANUAL = True
 X_AFTER, X_STEP = 1, 3
+GQ = 32
 A_BUFS = 8
 B_BUFS = 4
 
@@ -228,12 +229,22 @@ def tile_dbrxexpertglu_kernel(tc, x, expert_w1, expert_v1, expert_w2, out):
             rows = raw[("A", idx, m, c)][:].rearrange("p (j w) -> p j w", j=4)
             return rows[:, :, k * KP : (k + 1) * KP], grp[:]
 
-        def regroup_v(unit):
+        def regroup_v(unit, pool_pairs):
             src, dst = regroup_views(unit)
+            top = QS - pool_pairs // 2
             nc.vector.tensor_copy(
-                out=dst.rearrange("p (e c l j) -> p c j l e", e=2, l=2, j=4)[:, 0 : QS],
-                in_=src.rearrange("p j (c l e) -> p c j l e", l=2, e=2)[:, 0 : QS],
+                out=dst.rearrange("p (e c l j) -> p c j l e", e=2, l=2, j=4)[:, 0:top],
+                in_=src.rearrange("p j (c l e) -> p c j l e", l=2, e=2)[:, 0:top],
             )
+            if pool_pairs:
+                nc.gpsimd.tensor_scalar(
+                    out=dst.rearrange("p (e q j) -> p q j e", e=2, j=4)[:, 2 * top : 2 * QS],
+                    in0=src.rearrange("p j (q e) -> p q j e", e=2)[:, 2 * top : 2 * QS],
+                    scalar1=1.0,
+                    scalar2=0.0,
+                    op0=MULT,
+                    op1=mybir.AluOpType.add,
+                )
 
         def regroup_s(unit, part):
             src, dst = regroup_views(unit)
@@ -383,7 +394,7 @@ def tile_dbrxexpertglu_kernel(tc, x, expert_w1, expert_v1, expert_w2, out):
                 x_transpose()
             run(step, "pe_tr")
             if unit is not None:
-                regroup_v(unit)
+                regroup_v(unit, GQ if (step, "v_mul") in due else 0)
             run(step, "v_mul")
             if 1 <= step <= len(units):
                 quantise_a(units[step - 1])

@@ -25,7 +25,6 @@ QS = 80
 LAG_G, LAG_S, LAG_U, LAG_M, LAG_QH, LAG_QB, LAG_S2, TR_LEAD = 1, 1, 1, 2, 1, 1, 2, 1
 MANUAL = True
 X_AFTER, X_STEP = 1, 3
-GQ = 32
 A_BUFS = 8
 B_BUFS = 4
 
@@ -229,29 +228,18 @@ def tile_dbrxexpertglu_kernel(tc, x, expert_w1, expert_v1, expert_w2, out):
             rows = raw[("A", idx, m, c)][:].rearrange("p (j w) -> p j w", j=4)
             return rows[:, :, k * KP : (k + 1) * KP], grp[:]
 
-        def regroup_v(unit, pool_pairs):
+        def regroup_v(unit):
             src, dst = regroup_views(unit)
-            top = QS - pool_pairs // 2
             nc.vector.tensor_copy(
-                out=dst.rearrange("p (e c l j) -> p c j l e", e=2, l=2, j=4)[:, 0:top],
-                in_=src.rearrange("p j (c l e) -> p c j l e", l=2, e=2)[:, 0:top],
+                out=dst.rearrange("p (e c l j) -> p c j l e", e=2, l=2, j=4)[:, 0 : QS],
+                in_=src.rearrange("p j (c l e) -> p c j l e", l=2, e=2)[:, 0 : QS],
             )
-            if pool_pairs:
-                nc.gpsimd.tensor_scalar(
-                    out=dst.rearrange("p (e q j) -> p q j e", e=2, j=4)[:, 2 * top : 2 * QS],
-                    in0=src.rearrange("p j (q e) -> p q j e", e=2)[:, 2 * top : 2 * QS],
-                    scalar1=1.0,
-                    scalar2=0.0,
-                    op0=MULT,
-                    op1=mybir.AluOpType.add,
-                )
 
-        def regroup_s(unit, part):
+        def regroup_s(unit):
             src, dst = regroup_views(unit)
-            lo = 2 * QS + part * (P - QS)
             nc.scalar.copy(
-                out=dst.rearrange("p (e q j) -> p q j e", e=2, j=4)[:, lo : lo + P - QS],
-                in_=src.rearrange("p j (q e) -> p q j e", e=2)[:, lo : lo + P - QS],
+                out=dst.rearrange("p (e q j) -> p q j e", e=2, j=4)[:, 2 * QS : 2 * P],
+                in_=src.rearrange("p j (q e) -> p q j e", e=2)[:, 2 * QS : 2 * P],
             )
 
         def a_codes(idx, m):
@@ -394,7 +382,7 @@ def tile_dbrxexpertglu_kernel(tc, x, expert_w1, expert_v1, expert_w2, out):
                 x_transpose()
             run(step, "pe_tr")
             if unit is not None:
-                regroup_v(unit, GQ if (step, "v_mul") in due else 0)
+                regroup_v(unit)
             run(step, "v_mul")
             if 1 <= step <= len(units):
                 quantise_a(units[step - 1])
@@ -404,10 +392,8 @@ def tile_dbrxexpertglu_kernel(tc, x, expert_w1, expert_v1, expert_w2, out):
                     out=x_codes[:].bitcast(FP8X4), scales=x_scales[:], in_=x_grp[:]
                 )
             if unit is not None:
-                regroup_s(unit, 0)
+                regroup_s(unit)
             run(step, "s_ev")
-            if unit is not None:
-                regroup_s(unit, 1)
             run(step, "s_silu")
             if unit is not None and unit[5]:
                 live["A"] -= 1

@@ -21,10 +21,11 @@ B_CHUNKS = ((0, 2), (2, 2), (4, 2), (6, 1))
 B_AFTER = (5, 7, 9, 11, 12, 16, 16, 16)
 BANK_NUM, BANK_DEN = 2, 3
 DELTA = 0
-QS = 80
+QS = 88
 LAG_G, LAG_S, LAG_U, LAG_M, LAG_QH, LAG_QB, LAG_S2, TR_LEAD = 1, 1, 1, 2, 1, 1, 2, 1
 MANUAL = True
 X_AFTER, X_STEP = 1, 3
+GQ = 64
 A_BUFS = 8
 B_BUFS = 4
 
@@ -228,12 +229,22 @@ def tile_dbrxexpertglu_kernel(tc, x, expert_w1, expert_v1, expert_w2, out):
             rows = raw[("A", idx, m, c)][:].rearrange("p (j w) -> p j w", j=4)
             return rows[:, :, k * KP : (k + 1) * KP], grp[:]
 
-        def regroup_v(unit):
+        def regroup_v(unit, pool_pairs):
             src, dst = regroup_views(unit)
+            top = QS - pool_pairs // 2
             nc.vector.tensor_copy(
-                out=dst.rearrange("p (e c l j) -> p c j l e", e=2, l=2, j=4)[:, 0 : QS],
-                in_=src.rearrange("p j (c l e) -> p c j l e", l=2, e=2)[:, 0 : QS],
+                out=dst.rearrange("p (e c l j) -> p c j l e", e=2, l=2, j=4)[:, 0:top],
+                in_=src.rearrange("p j (c l e) -> p c j l e", l=2, e=2)[:, 0:top],
             )
+            if pool_pairs:
+                nc.gpsimd.tensor_scalar(
+                    out=dst.rearrange("p (e q j) -> p q j e", e=2, j=4)[:, 2 * top : 2 * QS],
+                    in0=src.rearrange("p j (q e) -> p q j e", e=2)[:, 2 * top : 2 * QS],
+                    scalar1=1.0,
+                    scalar2=0.0,
+                    op0=MULT,
+                    op1=mybir.AluOpType.add,
+                )
 
         def regroup_s(unit):
             src, dst = regroup_views(unit)
@@ -382,7 +393,7 @@ def tile_dbrxexpertglu_kernel(tc, x, expert_w1, expert_v1, expert_w2, out):
                 x_transpose()
             run(step, "pe_tr")
             if unit is not None:
-                regroup_v(unit)
+                regroup_v(unit, GQ if (step, "v_mul") in due else 0)
             run(step, "v_mul")
             if 1 <= step <= len(units):
                 quantise_a(units[step - 1])

@@ -25,7 +25,6 @@ QS = 88
 LAG_G, LAG_S, LAG_U, LAG_M, LAG_QH, LAG_QB, LAG_S2, TR_LEAD = 1, 1, 1, 2, 1, 1, 2, 1
 MANUAL = True
 X_AFTER, X_STEP = 1, 3
-GQ = 64
 A_BUFS = 8
 B_BUFS = 4
 
@@ -229,22 +228,12 @@ def tile_dbrxexpertglu_kernel(tc, x, expert_w1, expert_v1, expert_w2, out):
             rows = raw[("A", idx, m, c)][:].rearrange("p (j w) -> p j w", j=4)
             return rows[:, :, k * KP : (k + 1) * KP], grp[:]
 
-        def regroup_v(unit, pool_pairs):
+        def regroup_v(unit):
             src, dst = regroup_views(unit)
-            top = QS - pool_pairs // 2
             nc.vector.tensor_copy(
-                out=dst.rearrange("p (e c l j) -> p c j l e", e=2, l=2, j=4)[:, 0:top],
-                in_=src.rearrange("p j (c l e) -> p c j l e", l=2, e=2)[:, 0:top],
+                out=dst.rearrange("p (e c l j) -> p c j l e", e=2, l=2, j=4)[:, 0 : QS],
+                in_=src.rearrange("p j (c l e) -> p c j l e", l=2, e=2)[:, 0 : QS],
             )
-            if pool_pairs:
-                nc.gpsimd.tensor_scalar(
-                    out=dst.rearrange("p (e q j) -> p q j e", e=2, j=4)[:, 2 * top : 2 * QS],
-                    in0=src.rearrange("p j (q e) -> p q j e", e=2)[:, 2 * top : 2 * QS],
-                    scalar1=1.0,
-                    scalar2=0.0,
-                    op0=MULT,
-                    op1=mybir.AluOpType.add,
-                )
 
         def regroup_s(unit):
             src, dst = regroup_views(unit)
@@ -393,7 +382,7 @@ def tile_dbrxexpertglu_kernel(tc, x, expert_w1, expert_v1, expert_w2, out):
                 x_transpose()
             run(step, "pe_tr")
             if unit is not None:
-                regroup_v(unit, GQ if (step, "v_mul") in due else 0)
+                regroup_v(unit)
             run(step, "v_mul")
             if 1 <= step <= len(units):
                 quantise_a(units[step - 1])

from contextlib import ExitStack

import concourse.mybir as mybir
from concourse.masks import make_identity

F32 = mybir.dt.float32
BF16 = mybir.dt.bfloat16
U32 = mybir.dt.uint32
U8 = mybir.dt.uint8
FP8X4 = mybir.dt.float8_e4m3fn_x4
SILU = mybir.ActivationFunctionType.Silu
MULT = mybir.AluOpType.mult

P = 128
T, H, F = 256, 1024, 3584
KP = 512
NG = F // KP

A_CHUNKS = ((0, 2), (2, 2), (4, 2), (6, 1))
B_CHUNKS = ((0, 2), (2, 2), (4, 2), (6, 1))
B_AFTER = (5, 7, 9, 11, 12, 16, 16, 16)
BANK_NUM, BANK_DEN = 2, 3
DELTA = 0
QS = 88
LAG_G, LAG_S, LAG_U, LAG_M, LAG_QH, LAG_QB, LAG_S2, TR_LEAD = 1, 1, 1, 2, 1, 1, 2, 1
MANUAL = True
X_AFTER, X_STEP = 1, 3
A_BUFS = 8
B_BUFS = 4


def make_plan():
    pieces = []
    units = []
    first_step = []
    for idx, (g0, n) in enumerate(A_CHUNKS):
        for m in range(2):
            for c in range(2):
                pieces.append(("A", idx, m, c))
                first_step.append(len(units))
                for k in range(n):
                    units.append((idx, m, c, g0 + k, k, k == n - 1))
    first_step.append(len(units))
    b_pieces = []
    banks = []
    for idx, (g0, n) in enumerate(B_CHUNKS):
        for ob in range(2):
            b_pieces.append(("B", idx, ob, n))
            for k in range(n):
                for b in range(2):
                    banks.append((idx, g0 + k, k, ob, b, k == n - 1 and b == 1))
    loads = []
    nxt = 0
    for a in range(len(pieces) + 1):
        while nxt < len(b_pieces) and B_AFTER[nxt] == a:
            loads.append(b_pieces[nxt])
            nxt += 1
        if a < len(pieces):
            loads.append(pieces[a])
    bank_step = []
    cur = -1000000
    for j, piece in enumerate(b_pieces):
        cur = max(cur, (first_step[B_AFTER[j]] + DELTA) * BANK_DEN)
        for k in range(piece[3] * 2):
            bank_step.append(cur // BANK_DEN)
            cur += BANK_NUM

    due = {}

    def add(step, slot, op):
        if (step, slot) not in due:
            due[(step, slot)] = []
        due[(step, slot)].append(op)

    unit_step = {}
    for s, (idx, m, c, g, k, last) in enumerate(units):
        unit_step[(g, m, c)] = s
    silu_step = {}
    qh_step = {}
    prev = -9
    for g in range(NG):
        for th in range(2):
            gs = max(unit_step[(g, 0, 1)] + LAG_G, prev)
            add(gs, "pe_gate", ("GU", g, 0, th))
            prev = gs + LAG_S
            add(prev, "s_silu", ("SILU", g, th))
            silu_step[(g, th)] = prev
    prev = -9
    for g in range(NG):
        for th in range(2):
            us = max(unit_step[(g, 1, 1)] + LAG_U, prev, silu_step[(g, th)] - LAG_M)
            add(us, "pe_up", ("GU", g, 1, th))
            prev = us + LAG_M
            add(prev, "v_mul", ("MUL", g, th))
            add(prev + LAG_QH, "v_q", ("QH", g, th))
            qh_step[(g, th)] = prev + LAG_QH
    qb_step = {}
    for t, (idx, g, k, ob, b, last) in enumerate(banks):
        s = bank_step[t]
        early = bank_step[t - 2] + 1 if t >= 2 else -1
        add(max(s - TR_LEAD, early, -1), "pe_tr", ("TR", idx, g, k, ob, b, last))
        add(s, "s_ev", ("EV", g, ob, b))
        if b == 1:
            add(s + LAG_QB, "v_q", ("QB", g, ob))
            qb_step[(g, ob)] = s + LAG_QB
    last_s2 = {}
    for g in range(NG):
        for tt in range(2):
            for ob in range(2):
                s = max(qb_step[(g, ob)], qh_step[(g, tt)]) + LAG_S2
                s = max(s, last_s2.get((tt, ob), -99))
                last_s2[(tt, ob)] = s
                add(s, "pe_s2", ("S2", g, tt, ob))
    n_steps = max(step for step, slot in due) + 1
    return loads, units, due, n_steps


FLOPS = 2 * T * H * F * 3


def tile_dbrxexpertglu_kernel(tc, x, expert_w1, expert_v1, expert_w2, out):
    nc = tc.nc
    loads, units, due, n_steps = make_plan()
    with ExitStack() as ctx:
        keep = ctx.enter_context(tc.tile_pool(name="keep", bufs=1))
        araw_pool = ctx.enter_context(tc.tile_pool(name="araw", bufs=A_BUFS))
        braw_pool = ctx.enter_context(tc.tile_pool(name="braw", bufs=B_BUFS))
        agrp_pool = ctx.enter_context(tc.tile_pool(name="agrp", bufs=4))
        bgrp_pool = ctx.enter_context(tc.tile_pool(name="bgrp", bufs=3))
        acode_pool = ctx.enter_context(tc.tile_pool(name="acode", bufs=2))
        bcode_pool = ctx.enter_context(tc.tile_pool(name="bcode", bufs=3))
        sg_pool = ctx.enter_context(tc.tile_pool(name="sgp", bufs=4))
        hg_pool = ctx.enter_context(tc.tile_pool(name="hgp", bufs=2))
        ost_pool = ctx.enter_context(tc.tile_pool(name="ost", bufs=4))
        acc_pool = ctx.enter_context(tc.psum_pool(name="accp", bufs=1))
        gu_pool = ctx.enter_context(tc.psum_pool(name="gup", bufs=1))
        tr_pool = ctx.enter_context(tc.psum_pool(name="trp", bufs=2))
        if MANUAL:
            ctx.enter_context(tc.manual_schedule())

        ident = keep.tile([P, P], F32, name="ident")
        make_identity(nc, ident[:])


        raw = {}
        live = {"A": 0, "B": 0}
        limit = {"A": A_BUFS, "B": B_BUFS}
        issued = [0]

        def pump():
            while issued[0] < len(loads) and live[loads[issued[0]][0]] < limit[loads[issued[0]][0]]:
                kind, idx, second, third = loads[issued[0]]
                issued[0] += 1
                live[kind] += 1
                if kind == "A":
                    m, c = second, third
                    g0, n = A_CHUNKS[idx]
                    width = n * KP
                    w = expert_w1 if m == 0 else expert_v1
                    piece = araw_pool.tile([P, 4 * width], BF16, name="araw")
                    nc.sync.dma_start(
                        out=piece[:].rearrange("p (j w) -> p j w", j=4),
                        in_=w[c * KP : (c + 1) * KP, g0 * KP : g0 * KP + width].rearrange(
                            "(p j) w -> p j w", j=4
                        ),
                    )
                    raw[("A", idx, m, c)] = piece
                else:
                    ob = second
                    g0, n = B_CHUNKS[idx]
                    width = n * KP
                    piece = braw_pool.tile([P, 4 * width], BF16, name="braw")
                    nc.sync.dma_start(
                        out=piece[:].rearrange("p (o w) -> p o w", o=4),
                        in_=expert_w2[
                            ob * 512 : (ob + 1) * 512, g0 * KP : g0 * KP + width
                        ].rearrange("(o p) w -> p o w", p=P),
                    )
                    raw[("B", idx, ob)] = piece

        limit["A"] = X_AFTER
        pump()
        limit["A"] = A_BUFS
        x_raw = keep.tile([P, 2 * H], BF16, name="x_raw")
        nc.sync.dma_start(
            out=x_raw[:].rearrange("p (a k) -> p a k", a=2),
            in_=x.rearrange("(a p) k -> p a k", p=P),
        )
        pump()

        x_grp = keep.tile([P, 2 * T * 4], BF16, name="x_grp", align_bytes=64)
        x_codes = keep.tile([P, 2 * T], U32, name="x_codes", align_bytes=64)
        x_scales = keep.tile([P, 2 * T], U8, name="x_scales", align_bytes=64)
        x_words = x_raw[:].bitcast(F32).rearrange("p (a c m u) -> p a c u m", a=2, c=2, u=2)
        x_grp_words = x_grp[:].bitcast(F32)
        def x_transpose():
            for c in range(2):
                bank = tr_pool.tile([P, 512], F32, name="tr")
                for a in range(2):
                    for u in range(2):
                        s = a * 2 + u
                        nc.tensor.transpose(
                            bank[:, s * P : (s + 1) * P], x_words[:, a, c, u, :], ident[:]
                        )
                nc.scalar.copy(
                    out=x_grp_words[:, c * 512 : (c + 1) * 512].rearrange(
                        "p (a t u) -> p a t u", a=2, u=2
                    ),
                    in_=bank[:].rearrange("p (a u t) -> p a t u", a=2, u=2),
                )

        h_codes = keep.tile([P, NG * T], U32, name="h_codes", align_bytes=64)
        h_scales = keep.tile([P, NG * T], U8, name="h_scales", align_bytes=64)
        acc = [
            [acc_pool.tile([P, 512], F32, name="acc%d%d" % (tt, ob)) for ob in range(2)]
            for tt in range(2)
        ]

        tiles = {}

        def regroup_views(unit):
            idx, m, c, g, k, last = unit
            if ("agrp", g, m, c) not in tiles:
                tiles[("agrp", g, m, c)] = agrp_pool.tile(
                    [P, 4 * KP], BF16, name="agrp", align_bytes=64
                )
            grp = tiles[("agrp", g, m, c)]
            rows = raw[("A", idx, m, c)][:].rearrange("p (j w) -> p j w", j=4)
            return rows[:, :, k * KP : (k + 1) * KP], grp[:]

        def regroup_v(unit):
            src, dst = regroup_views(unit)
            nc.vector.tensor_copy(
                out=dst.rearrange("p (e c l j) -> p c j l e", e=2, l=2, j=4)[:, 0 : QS],
                in_=src.rearrange("p j (c l e) -> p c j l e", l=2, e=2)[:, 0 : QS],
            )

        def regroup_s(unit):
            src, dst = regroup_views(unit)
            nc.scalar.copy(
                out=dst.rearrange("p (e q j) -> p q j e", e=2, j=4)[:, 2 * QS : 2 * P],
                in_=src.rearrange("p j (q e) -> p q j e", e=2)[:, 2 * QS : 2 * P],
            )

        def a_codes(idx, m):
            n = A_CHUNKS[idx][1]
            if ("acodes", idx, m) not in tiles:
                tiles[("acodes", idx, m)] = acode_pool.tile(
                    [P, 2 * n * KP], U32, name="acodes%d" % m, align_bytes=64
                )
                tiles[("ascales", idx, m)] = acode_pool.tile(
                    [P, 2 * n * KP], U8, name="ascales%d" % m, align_bytes=64
                )
            return tiles[("acodes", idx, m)], tiles[("ascales", idx, m)], n

        def quantise_a(unit):
            idx, m, c, g, k, last = unit
            codes, scales, n = a_codes(idx, m)
            col = (c * n + k) * KP
            nc.vector.quantize_mx(
                out=codes[:, col : col + KP].bitcast(FP8X4),
                scales=scales[:, col : col + KP],
                in_=tiles[("agrp", g, m, c)][:],
            )

        chunk_of = {}
        for idx, (g0, n) in enumerate(A_CHUNKS):
            for k in range(n):
                chunk_of[g0 + k] = (idx, k)

        def emit(op):
            kind = op[0]
            if kind == "GU":
                g, m, th = op[1:]
                idx, k = chunk_of[g]
                codes, scales, n = a_codes(idx, m)
                bank = gu_pool.tile([P, 512], F32, name="gate" if m == 0 else "up")
                tiles[("gu", g, m, th)] = bank
                for j4 in range(4):
                    for c in range(2):
                        col = (c * n + k) * KP + ((j4 % 2) * 2 + j4 // 2) * P
                        xcol = c * T + th * P
                        nc.tensor.matmul_mx(
                            out=bank[:, j4 * P : (j4 + 1) * P],
                            lhsT=codes[:, col : col + P].bitcast(FP8X4),
                            lhsT_scale=scales[:, col : col + P],
                            rhs=x_codes[:, xcol : xcol + P].bitcast(FP8X4),
                            rhs_scale=x_scales[:, xcol : xcol + P],
                            start=(c == 0),
                            stop=(c == 1),
                        )
            elif kind == "SILU":
                g, th = op[1:]
                sg = sg_pool.tile([P, 512], F32, name="sg")
                tiles[("sg", g, th)] = sg
                nc.scalar.activation(
                    out=sg[:].rearrange("p (t j) -> p t j", j=4),
                    in_=tiles[("gu", g, 0, th)][:].rearrange("p (j t) -> p t j", j=4),
                    func=SILU,
                )
            elif kind == "MUL":
                g, th = op[1:]
                if th == 0:
                    tiles[("hg", g)] = hg_pool.tile([P, 2 * 512], BF16, name="hg", align_bytes=64)
                nc.vector.tensor_tensor(
                    out=tiles[("hg", g)][:, th * 512 : (th + 1) * 512].rearrange(
                        "p (t j) -> p t j", j=4
                    ),
                    in0=tiles[("sg", g, th)][:].rearrange("p (t j) -> p t j", j=4),
                    in1=tiles[("gu", g, 1, th)][:].rearrange("p (j t) -> p t j", j=4),
                    op=MULT,
                )
            elif kind == "QH":
                g, th = op[1:]
                col = g * T + th * P
                nc.vector.quantize_mx(
                    out=h_codes[:, col : col + P].bitcast(FP8X4),
                    scales=h_scales[:, col : col + P],
                    in_=tiles[("hg", g)][:, th * 512 : (th + 1) * 512],
                )
            elif kind == "TR":
                idx, g, k, ob, b, last = op[1:]
                half = B_CHUNKS[idx][1] * KP // 2
                words = raw[("B", idx, ob)][:].bitcast(F32)
                bank = tr_pool.tile([P, 512], F32, name="tr")
                tiles[("tr", g, ob, b)] = bank
                for a in range(2):
                    for u in range(2):
                        s = a * 2 + u
                        first = (b * 2 + a) * half + k * 256 + u * P
                        nc.tensor.transpose(
                            bank[:, s * P : (s + 1) * P], words[:, first : first + P], ident[:]
                        )
                if last:
                    live["B"] -= 1
            elif kind == "EV":
                g, ob, b = op[1:]
                if b == 0:
                    tiles[("bgrp", g, ob)] = bgrp_pool.tile(
                        [P, 2048], BF16, name="bgrp", align_bytes=64
                    )
                nc.scalar.copy(
                    out=tiles[("bgrp", g, ob)][:]
                    .bitcast(F32)[:, b * 512 : (b + 1) * 512]
                    .rearrange("p (a o u) -> p a o u", a=2, u=2),
                    in_=tiles[("tr", g, ob, b)][:].rearrange("p (a u o) -> p a o u", a=2, u=2),
                )
            elif kind == "QB":
                g, ob = op[1:]
                if ("bcodes", g) not in tiles:
                    tiles[("bcodes", g)] = bcode_pool.tile(
                        [P, 1024], U32, name="bcodes", align_bytes=64
                    )
                    tiles[("bscales", g)] = bcode_pool.tile(
                        [P, 1024], U8, name="bscales", align_bytes=64
                    )
                nc.vector.quantize_mx(
                    out=tiles[("bcodes", g)][:, ob * 512 : (ob + 1) * 512].bitcast(FP8X4),
                    scales=tiles[("bscales", g)][:, ob * 512 : (ob + 1) * 512],
                    in_=tiles[("bgrp", g, ob)][:],
                )
            else:
                g, tt, ob = op[1:]
                hcol = g * T + tt * P
                nc.tensor.matmul_mx(
                    out=acc[tt][ob][:],
                    lhsT=h_codes[:, hcol : hcol + P].bitcast(FP8X4),
                    lhsT_scale=h_scales[:, hcol : hcol + P],
                    rhs=tiles[("bcodes", g)][:, ob * 512 : (ob + 1) * 512].bitcast(FP8X4),
                    rhs_scale=tiles[("bscales", g)][:, ob * 512 : (ob + 1) * 512],
                    start=(g == 0),
                    stop=(g == NG - 1),
                )

        def run(step, slot):
            for op in due.get((step, slot), []):
                emit(op)

        for step in range(-1, n_steps):
            unit = units[step] if 0 <= step < len(units) else None
            if step == X_STEP - 1:
                x_transpose()
            run(step, "pe_tr")
            if unit is not None:
                regroup_v(unit)
            run(step, "v_mul")
            if 1 <= step <= len(units):
                quantise_a(units[step - 1])
            run(step, "v_q")
            if step == X_STEP:
                nc.vector.quantize_mx(
                    out=x_codes[:].bitcast(FP8X4), scales=x_scales[:], in_=x_grp[:]
                )
            if unit is not None:
                regroup_s(unit)
            run(step, "s_ev")
            run(step, "s_silu")
            if unit is not None and unit[5]:
                live["A"] -= 1
            run(step, "pe_s2")
            run(step, "pe_up")
            run(step, "pe_gate")
            pump()

        for tt in range(2):
            for ob in range(2):
                res = ost_pool.tile([P, 512], F32, name="res")
                copy = nc.vector.tensor_copy if ob == 0 else nc.scalar.copy
                copy(out=res[:], in_=acc[tt][ob][:])
                nc.sync.dma_start(
                    out=out[tt * P : (tt + 1) * P, ob * 512 : (ob + 1) * 512], in_=res[:]
                )
